import numpy as np
import ml_dtypes


def mxq(x, axis, fmt="e4m3"):
    dtype, down = {"e4m3": (ml_dtypes.float8_e4m3fn, 7), "e5m2": (ml_dtypes.float8_e5m2, 14)}[fmt]
    v = np.moveaxis(np.asarray(x, np.float32).astype(ml_dtypes.bfloat16).astype(np.float64), axis, -1)
    blocks = v.reshape(v.shape[:-1] + (-1, 32))
    amax = np.abs(blocks).max(-1, keepdims=True)
    byte = np.maximum(np.where(amax > 0, np.frexp(amax)[1] - 1 + 127, 0) - down, 1)
    scale = np.exp2(byte - 127.0)
    codes = (blocks / scale).astype(np.float32).astype(dtype).astype(np.float64)
    return np.moveaxis((codes * scale).reshape(v.shape), -1, axis)


WIDE = False


def mx_kscale(k):
    if not WIDE:
        return np.ones(k)
    levels = np.array([10, -10, 5, -5, 0])
    if k % 512:
        return np.exp2(np.random.permutation(np.resize(levels, k // 32))).repeat(32)
    a = np.empty((k // 512, 16))
    for p in range(k // 512):
        a[p, :8] = np.random.permutation(np.resize(levels, 8))
        for g in range(8):
            far = levels[np.abs(levels - a[p, g]) >= 10]
            a[p, g + 8] = far[np.random.randint(len(far))]
    return np.exp2(a.ravel()).repeat(32)


BF16 = ml_dtypes.bfloat16


def bf(x):
    return np.asarray(x, np.float32).astype(BF16)


def f64(x):
    return np.asarray(x).astype(np.float64)


B, L, D = 3, 2048, 2048
SIG = 2.0


def setup_inputs():
    s, t = mx_kscale(D), mx_kscale(D)
    return {"x1": bf(np.random.standard_normal((B, L, D)) * s),
            "bi_linear_w": bf(np.random.standard_normal((D, D)) * SIG / D / s[:, None] * t),
            "x2": bf(np.random.standard_normal((B, L, D)) / t)}


def reference(x1, bi_linear_w, x2):
    h = mxq(f64(x1), 2, "e4m3") @ mxq(f64(bi_linear_w), 0, "e4m3")
    return mxq(h, 2, "e4m3") @ mxq(f64(x2), 2, "e4m3").transpose(0, 2, 1)

@@ -1,0 +1,302 @@
+from contextlib import ExitStack
+
+import concourse.mybir as mybir
+from concourse.masks import make_identity
+
+B, L, D = 3, 2048, 2048
+FLOPS = 2 * 2 * B * L * D * D
+
+F32 = mybir.dt.float32
+BF16 = mybir.dt.bfloat16
+U32 = mybir.dt.uint32
+U8 = mybir.dt.uint8
+FP8X4 = mybir.dt.float8_e4m3fn_x4
+
+P = 128
+CH = 512
+NG = 4
+NCH = L // CH
+
+
+def tile_coattentionandcombine_pa_l_kernel(tc, x1, bi_linear_w, x2, out):
+    nc = tc.nc
+    xs = (x1, x2)
+
+    with ExitStack() as ctx:
+        const = ctx.enter_context(tc.tile_pool(name="const", bufs=1))
+        keep = ctx.enter_context(tc.tile_pool(name="keep", bufs=1))
+        codes_pool = ctx.enter_context(tc.tile_pool(name="codes", bufs=12))
+        raw_pool = ctx.enter_context(tc.tile_pool(name="raw", bufs=4))
+        srt_pool = ctx.enter_context(tc.tile_pool(name="srt", bufs=2))
+        g_pool = ctx.enter_context(tc.tile_pool(name="grouped", bufs=5))
+        hb_pool = ctx.enter_context(tc.tile_pool(name="hb", bufs=2))
+        ob_pool = ctx.enter_context(tc.tile_pool(name="ob", bufs=2))
+        tp_pool = ctx.enter_context(tc.psum_pool(name="tp", bufs=4))
+        mm_pool = ctx.enter_context(tc.psum_pool(name="mm", bufs=4))
+        ctx.enter_context(tc.manual_schedule())
+
+        ident = const.tile([P, P], F32, name="ident")
+        make_identity(nc, ident[:])
+
+        w_codes = keep.tile([P, NG, NG, CH], U32, name="w_codes", align_bytes=64)
+        w_planes = keep.tile([P, NG, CH], U8, name="w_planes", align_bytes=64)
+
+        raws = {}
+        srts = {}
+        banks = {}
+        groupeds = {}
+        chunk_codes = {}
+        w_raws = {}
+
+        def new_codes(key):
+            c = codes_pool.tile([P, NG, CH], U32, name="codes", tag="codes", align_bytes=64)
+            s = codes_pool.tile([P, CH], U8, name="planes", tag="planes", align_bytes=64)
+            chunk_codes[key] = (c, s)
+            return chunk_codes[key]
+
+        def load(u):
+            which, ci, hf = u
+            b, c = divmod(ci, NCH)
+            raw = raw_pool.tile([P, 4, 1024], BF16, name="raw", tag="raw")
+            nc.sync.dma_start(
+                out=raw[:],
+                in_=xs[which][b, c * CH : (c + 1) * CH, hf * 1024 : (hf + 1) * 1024].rearrange(
+                    "(s p) k -> p s k", p=P
+                ),
+            )
+            raws[u] = raw
+
+        def sort_words(u):
+            words = raws.pop(u)[:].bitcast(F32)
+            srt = srt_pool.tile([P, 2, 4, 2, P], F32, name="srt", tag="srt")
+            for gg in range(2):
+                nc.vector.tensor_copy(
+                    out=srt[:, gg],
+                    in_=words[:, :, gg * 256 : (gg + 1) * 256].rearrange("p s (q u) -> p s u q", u=2),
+                )
+            srts[u] = srt
+
+        def transposes(u):
+            srt = srts.pop(u)
+            got = []
+            for gg in range(2):
+                for sp in range(2):
+                    tp = tp_pool.tile([P, 2, 2, P], F32, name="tp", tag="tp")
+                    for s2 in range(2):
+                        for uu in range(2):
+                            nc.tensor.transpose(tp[:, s2, uu, :], srt[:, gg, 2 * sp + s2, uu, :], ident[:])
+                    got.append(tp)
+            banks[u] = got
+
+        def evac_transposes(u):
+            got = banks.pop(u)
+            tiles = []
+            for gg in range(2):
+                g_t = g_pool.tile([P, 4 * CH], BF16, name="grouped", tag="g", align_bytes=64)
+                gw = g_t[:].bitcast(F32).rearrange("p (s c u) -> p s c u", s=4, u=2)
+                for sp in range(2):
+                    nc.scalar.copy(
+                        out=gw[:, 2 * sp : 2 * sp + 2],
+                        in_=got[2 * gg + sp][:].rearrange("p s u c -> p s c u"),
+                    )
+                tiles.append(g_t)
+            groupeds[u] = tiles
+
+        def quantise_unit(u):
+            which, ci, hf = u
+            if hf == 0:
+                new_codes((which, ci))
+            c, s = chunk_codes[(which, ci)]
+            tiles = groupeds.pop(u)
+            for gg in range(2):
+                g = 2 * hf + gg
+                nc.vector.quantize_mx(
+                    out=c[:, g, :].bitcast(FP8X4), scales=s[4 * g : P, :], in_=tiles[gg][:]
+                )
+
+        def load_w(g2):
+            for half in range(2):
+                w_raw = codes_pool.tile([P, 2, 4, CH], BF16, name="w_raw", tag="codes", align_bytes=64)
+                for k2 in range(2):
+                    gk = 2 * half + k2
+                    nc.sync.dma_start(
+                        out=w_raw[:, k2],
+                        in_=bi_linear_w[
+                            gk * 512 : (gk + 1) * 512, g2 * CH : (g2 + 1) * CH
+                        ].rearrange("(p j) c -> p j c", j=4),
+                    )
+                w_raws[(g2, half)] = w_raw
+
+        def interleave_w(g2, gk, engine_copy):
+            w_raw = w_raws[(g2, gk // 2)]
+            w_g = g_pool.tile([P, 4 * CH], BF16, name="w_grouped", tag="g", align_bytes=64)
+            engine_copy(
+                out=w_g[:].rearrange("p (t m j) -> p t m j", t=4, j=4),
+                in_=w_raw[:, gk % 2].rearrange("p j (m t) -> p t m j", t=4),
+            )
+            groupeds[("w", g2, gk)] = w_g
+
+        def quantise_w(g2, gk):
+            w_g = groupeds.pop(("w", g2, gk))
+            nc.vector.quantize_mx(
+                out=w_codes[:, gk, g2, :].bitcast(FP8X4),
+                scales=w_planes[4 * gk : P, g2, :],
+                in_=w_g[:],
+            )
+
+        def stage1_slot(ci, g2, mid):
+            xc, xp = chunk_codes[(0, ci)]
+            hb = hb_pool.tile([P, 4, CH], BF16, name="hb", tag="hb")
+            for t in range(4):
+                acc = mm_pool.tile([P, CH], F32, name="acc", tag="acc")
+                for gk in range(NG):
+                    nc.tensor.matmul_mx(
+                        out=acc[:],
+                        lhsT=w_codes[:, gk, g2, t * P : (t + 1) * P].bitcast(FP8X4),
+                        lhsT_scale=w_planes[4 * gk : P, g2, t * P : (t + 1) * P],
+                        rhs=xc[:, gk, :].bitcast(FP8X4),
+                        rhs_scale=xp[4 * gk : P, :],
+                        start=(gk == 0),
+                        stop=(gk == NG - 1),
+                    )
+                nc.scalar.copy(out=hb[:, t, :], in_=acc[:])
+                if t == 1 and mid is not None:
+                    mid()
+            return hb
+
+        def interleave_h(hb):
+            h_g = g_pool.tile([P, 4 * CH], BF16, name="h_grouped", tag="g", align_bytes=64)
+            nc.vector.tensor_copy(
+                out=h_g[:].rearrange("p (c t) -> p c t", t=4), in_=hb[:].rearrange("p t c -> p c t")
+            )
+            return h_g
+
+        def quantise_h(ci, g2, h_g):
+            if (2, ci) not in chunk_codes:
+                new_codes((2, ci))
+            c, s = chunk_codes[(2, ci)]
+            nc.vector.quantize_mx(out=c[:, g2, :].bitcast(FP8X4), scales=s[4 * g2 : P, :], in_=h_g[:])
+
+        def stage2_slot(ci, mc, last):
+            b, lc = divmod(ci, NCH)
+            hc, hp = chunk_codes[(2, ci)]
+            xc, xp = chunk_codes[(1, b * NCH + mc)]
+            ob = ob_pool.tile([P, 4, CH], F32, name="ob", tag="ob")
+            dst = out[b, lc * CH : (lc + 1) * CH, mc * CH : (mc + 1) * CH].rearrange("(t p) m -> p t m", p=P)
+            for lt in range(4):
+                acc = mm_pool.tile([P, CH], F32, name="acc", tag="acc")
+                for g2 in range(NG):
+                    nc.tensor.matmul_mx(
+                        out=acc[:],
+                        lhsT=hc[:, g2, lt * P : (lt + 1) * P].bitcast(FP8X4),
+                        lhsT_scale=hp[4 * g2 : P, lt * P : (lt + 1) * P],
+                        rhs=xc[:, g2, :].bitcast(FP8X4),
+                        rhs_scale=xp[4 * g2 : P, :],
+                        start=(g2 == 0),
+                        stop=(g2 == NG - 1),
+                    )
+                nc.scalar.copy(out=ob[:, lt, :], in_=acc[:])
+                if last:
+                    nc.sync.dma_start(out=dst[:, lt, :], in_=ob[:, lt, :])
+            if not last:
+                nc.sync.dma_start(out=dst, in_=ob[:])
+
+        def both(which, chunks):
+            return [(which, ci, hf) for ci in chunks for hf in range(2)]
+
+        slots = []
+        after = {}
+        units = both(0, [0, 1])
+        n_head = len(units)
+        for b in range(B):
+            base = len(slots)
+            c0 = b * NCH
+            if b == 0:
+                slots.extend([(1, ci, g2) for g2 in range(NG) for ci in (0, 1)])
+                slots.extend([(1, ci, g2) for ci in (2, 3) for g2 in range(NG)])
+                todo = both(0, [2, 3]) + both(1, [0, 1, 2, 3])
+                first = base + 4
+            else:
+                slots.extend([(1, c0 + lc, g2) for lc in range(NCH) for g2 in range(NG)])
+                todo = both(1, [c0 + 2, c0 + 3])
+                first = base
+            for k in range(len(todo)):
+                after[first + k] = len(units) + k
+            units.extend(todo)
+            base = len(slots)
+            slots.extend([(2, c0 + lc, mc) for lc in range(NCH) for mc in range(NCH)])
+            if b + 1 < B:
+                n0 = c0 + NCH
+                todo = both(0, [n0, n0 + 1, n0 + 2, n0 + 3]) + both(1, [n0, n0 + 1])
+                for k in range(len(todo)):
+                    after[base + k] = len(units) + k
+                units.extend(todo)
+
+        def sort_and_refill(k):
+            sort_words(units[k])
+            if k + 4 < len(units):
+                load(units[k + 4])
+
+        load(units[0])
+        load(units[1])
+        load_w(0)
+        load(units[2])
+        load(units[3])
+        for g2 in range(1, NG):
+            load_w(g2)
+        sort_and_refill(0)
+        sort_and_refill(1)
+        transposes(units[0])
+        evac_transposes(units[0])
+        transposes(units[1])
+        evac_transposes(units[1])
+        interleave_w(0, 0, nc.vector.tensor_copy)
+        quantise_unit(units[0])
+        interleave_w(0, 1, nc.scalar.copy)
+        interleave_w(0, 2, nc.vector.tensor_copy)
+        quantise_unit(units[1])
+        interleave_w(0, 3, nc.scalar.copy)
+        quantise_w(0, 0)
+        quantise_w(0, 2)
+        sort_and_refill(2)
+        transposes(units[2])
+        evac_transposes(units[2])
+        quantise_w(0, 1)
+        sort_and_refill(3)
+        transposes(units[3])
+        evac_transposes(units[3])
+        quantise_w(0, 3)
+        quantise_unit(units[2])
+        quantise_unit(units[3])
+
+        for n in range(len(slots)):
+            kind, ci, sub = slots[n]
+            w_job = None
+            if n < 2 * (NG - 1):
+                w_job = (n // 2 + 1, 2 * (n % 2))
+            if w_job is not None:
+                interleave_w(w_job[0], w_job[1], nc.vector.tensor_copy)
+            if (n + 1) in after:
+                sort_and_refill(after[n + 1])
+            if w_job is not None:
+                quantise_w(w_job[0], w_job[1])
+
+            if kind == 1:
+                mid = None
+                if w_job is not None:
+                    mid = lambda wj=w_job: interleave_w(wj[0], wj[1] + 1, nc.scalar.copy)
+                hb = stage1_slot(ci, sub, mid)
+            else:
+                stage2_slot(ci, sub, n == len(slots) - 1)
+            if w_job is not None:
+                quantise_w(w_job[0], w_job[1] + 1)
+
+            if n in after:
+                transposes(units[after[n]])
+                evac_transposes(units[after[n]])
+            if kind == 1:
+                h_g = interleave_h(hb)
+            if n in after:
+                quantise_unit(units[after[n]])
+            if kind == 1:
+                quantise_h(ci, sub, h_g)

@@ -13,9 +13,13 @@ U8 = mybir.dt.uint8
 FP8X4 = mybir.dt.float8_e4m3fn_x4
 
 P = 128
+Q = 32
 CH = 512
+UT = 256
 NG = 4
 NCH = L // CH
+PE_WAY = 0
+DVE_WAY = 1
 
 
 def tile_coattentionandcombine_pa_l_kernel(tc, x1, bi_linear_w, x2, out):
@@ -25,14 +29,12 @@ def tile_coattentionandcombine_pa_l_kernel(tc, x1, bi_linear_w, x2, out):
     with ExitStack() as ctx:
         const = ctx.enter_context(tc.tile_pool(name="const", bufs=1))
         keep = ctx.enter_context(tc.tile_pool(name="keep", bufs=1))
-        codes_pool = ctx.enter_context(tc.tile_pool(name="codes", bufs=12))
-        raw_pool = ctx.enter_context(tc.tile_pool(name="raw", bufs=4))
-        srt_pool = ctx.enter_context(tc.tile_pool(name="srt", bufs=2))
-        g_pool = ctx.enter_context(tc.tile_pool(name="grouped", bufs=5))
+        codes_pool = ctx.enter_context(tc.tile_pool(name="codes", bufs=11))
+        x_pool = ctx.enter_context(tc.tile_pool(name="xprep", bufs=8))
+        g_pool = ctx.enter_context(tc.tile_pool(name="grouped", bufs=4))
         hb_pool = ctx.enter_context(tc.tile_pool(name="hb", bufs=2))
         ob_pool = ctx.enter_context(tc.tile_pool(name="ob", bufs=2))
-        tp_pool = ctx.enter_context(tc.psum_pool(name="tp", bufs=4))
-        mm_pool = ctx.enter_context(tc.psum_pool(name="mm", bufs=4))
+        psum = ctx.enter_context(tc.psum_pool(name="psum", bufs=8))
         ctx.enter_context(tc.manual_schedule())
 
         ident = const.tile([P, P], F32, name="ident")
@@ -41,10 +43,7 @@ def tile_coattentionandcombine_pa_l_kernel(tc, x1, bi_linear_w, x2, out):
         w_codes = keep.tile([P, NG, NG, CH], U32, name="w_codes", align_bytes=64)
         w_planes = keep.tile([P, NG, CH], U8, name="w_planes", align_bytes=64)
 
-        raws = {}
-        srts = {}
-        banks = {}
-        groupeds = {}
+        stage = {}
         chunk_codes = {}
         w_raws = {}
 
@@ -52,117 +51,169 @@ def tile_coattentionandcombine_pa_l_kernel(tc, x1, bi_linear_w, x2, out):
             c = codes_pool.tile([P, NG, CH], U32, name="codes", tag="codes", align_bytes=64)
             s = codes_pool.tile([P, CH], U8, name="planes", tag="planes", align_bytes=64)
             chunk_codes[key] = (c, s)
-            return chunk_codes[key]
+
+        def x_tile(shape, dtype):
+            return x_pool.tile(shape, dtype, name="xt", tag="xt", align_bytes=64)
+
+        def bank():
+            return psum.tile([P, CH], F32, name="bank", tag="bank")
+
+        def quadrant_queue(a):
+            return (nc.sync, nc.scalar)[a // 2]
 
         def load(u):
-            which, ci, hf = u
+            which, ci, hf, way = u
             b, c = divmod(ci, NCH)
-            raw = raw_pool.tile([P, 4, 1024], BF16, name="raw", tag="raw")
-            nc.sync.dma_start(
-                out=raw[:],
-                in_=xs[which][b, c * CH : (c + 1) * CH, hf * 1024 : (hf + 1) * 1024].rearrange(
-                    "(s p) k -> p s k", p=P
-                ),
-            )
-            raws[u] = raw
-
-        def sort_words(u):
-            words = raws.pop(u)[:].bitcast(F32)
-            srt = srt_pool.tile([P, 2, 4, 2, P], F32, name="srt", tag="srt")
-            for gg in range(2):
-                nc.vector.tensor_copy(
-                    out=srt[:, gg],
-                    in_=words[:, :, gg * 256 : (gg + 1) * 256].rearrange("p s (q u) -> p s u q", u=2),
+            t0 = c * CH + hf * UT
+            if way == PE_WAY:
+                raw = x_tile([P, 2, D], BF16)
+                nc.sync.dma_start(
+                    out=raw[:], in_=xs[which][b, t0 : t0 + UT, :].rearrange("(s p) k -> p s k", p=P)
                 )
-            srts[u] = srt
-
-        def transposes(u):
-            srt = srts.pop(u)
-            got = []
-            for gg in range(2):
-                for sp in range(2):
-                    tp = tp_pool.tile([P, 2, 2, P], F32, name="tp", tag="tp")
-                    for s2 in range(2):
-                        for uu in range(2):
-                            nc.tensor.transpose(tp[:, s2, uu, :], srt[:, gg, 2 * sp + s2, uu, :], ident[:])
-                    got.append(tp)
-            banks[u] = got
-
-        def evac_transposes(u):
-            got = banks.pop(u)
-            tiles = []
-            for gg in range(2):
-                g_t = g_pool.tile([P, 4 * CH], BF16, name="grouped", tag="g", align_bytes=64)
-                gw = g_t[:].bitcast(F32).rearrange("p (s c u) -> p s c u", s=4, u=2)
-                for sp in range(2):
-                    nc.scalar.copy(
-                        out=gw[:, 2 * sp : 2 * sp + 2],
-                        in_=got[2 * gg + sp][:].rearrange("p s u c -> p s c u"),
+            else:
+                raw = x_tile([P, 8, CH], BF16)
+                for a in range(4):
+                    quadrant_queue(a).dma_start(
+                        out=raw[a * Q : (a + 1) * Q],
+                        in_=xs[which][b, t0 : t0 + UT, a * CH : (a + 1) * CH].rearrange(
+                            "(s j) k -> j s k", j=Q
+                        ),
                     )
-                tiles.append(g_t)
-            groupeds[u] = tiles
+            stage[("raw", u)] = raw
+
+        def stage_a(u):
+            raw = stage.pop(("raw", u))
+            srt = x_tile([P, 2048], F32)
+            if u[3] == PE_WAY:
+                words = raw[:].bitcast(F32)
+                dst = srt[:].rearrange("p (s r) -> p s r", s=2)
+                for s2 in range(2):
+                    nc.vector.tensor_copy(
+                        out=dst[:, s2, :].rearrange("p (g u a i) -> p g u a i", g=4, u=2, a=4),
+                        in_=words[:, s2, :].rearrange("p (a g i u) -> p g u a i", a=4, g=4, u=2),
+                    )
+            else:
+                words = raw[:].rearrange("p s k -> p (s k)").bitcast(F32)
+                nc.scalar.copy(
+                    out=srt[:].rearrange("p (r u i) -> p r u i", u=2, i=Q),
+                    in_=words.rearrange("p (r i u) -> p r u i", i=Q, u=2),
+                )
+            stage[("srt", u)] = srt
+
+        def pe_transposes(u):
+            srt = stage.pop(("srt", u))[:].rearrange("p (s g u q) -> p s g u q", s=2, g=4, u=2)
+            grouped = x_tile([P, NG, 4 * UT], BF16)
+            gw = grouped[:].bitcast(F32)
+            got = []
+            for g in range(NG):
+                tp = bank()
+                tpv = tp[:].rearrange("p (s u c) -> p s u c", s=2, u=2)
+                for s2 in range(2):
+                    for uu in range(2):
+                        nc.tensor.transpose(tpv[:, s2, uu, :], srt[:, s2, g, uu, :], ident[:])
+                got.append(tpv)
+            for g in range(NG):
+                nc.scalar.copy(
+                    out=gw[:, g, :].rearrange("p (s c u) -> p s c u", s=2, u=2),
+                    in_=got[g].rearrange("p s u c -> p s c u"),
+                )
+            stage[("grouped", u)] = grouped
+
+        def dve_transpose(u):
+            srt = stage.pop(("srt", u))
+            turned = x_tile([P, 2048], F32)
+            nc.vector.transpose(out=turned[:], in_=srt[:])
+            stage[("turned", u)] = turned
+
+        def dve_regroup(u):
+            turned = stage.pop(("turned", u))
+            grouped = x_tile([P, NG, 4 * UT], BF16)
+            nc.vector.tensor_copy(
+                out=grouped[:].bitcast(F32).rearrange("p g (s j u) -> p g s j u", s=8, u=2),
+                in_=turned[:].rearrange("p (s g u j) -> p g s j u", s=8, g=4, u=2),
+            )
+            stage[("grouped", u)] = grouped
 
         def quantise_unit(u):
-            which, ci, hf = u
+            which, ci, hf, way = u
             if hf == 0:
                 new_codes((which, ci))
             c, s = chunk_codes[(which, ci)]
-            tiles = groupeds.pop(u)
-            for gg in range(2):
-                g = 2 * hf + gg
+            grouped = stage.pop(("grouped", u))
+            for g in range(NG):
                 nc.vector.quantize_mx(
-                    out=c[:, g, :].bitcast(FP8X4), scales=s[4 * g : P, :], in_=tiles[gg][:]
+                    out=c[:, g, hf * UT : (hf + 1) * UT].bitcast(FP8X4),
+                    scales=s[4 * g : P, hf * UT : (hf + 1) * UT],
+                    in_=grouped[:, g, :],
                 )
 
-        def load_w(g2):
-            for half in range(2):
-                w_raw = codes_pool.tile([P, 2, 4, CH], BF16, name="w_raw", tag="codes", align_bytes=64)
-                for k2 in range(2):
-                    gk = 2 * half + k2
-                    nc.sync.dma_start(
-                        out=w_raw[:, k2],
-                        in_=bi_linear_w[
-                            gk * 512 : (gk + 1) * 512, g2 * CH : (g2 + 1) * CH
-                        ].rearrange("(p j) c -> p j c", j=4),
+        def load_w(gk):
+            for h in range(2):
+                w_raw = codes_pool.tile([P, 4, 1024], BF16, name="w_raw", tag="codes", align_bytes=64)
+                for a in range(4):
+                    r0 = a * 512 + gk * P
+                    quadrant_queue(a).dma_start(
+                        out=w_raw[a * Q : (a + 1) * Q],
+                        in_=bi_linear_w[r0 : r0 + P, h * 1024 : (h + 1) * 1024].rearrange(
+                            "(i j) c -> i j c", j=4
+                        ),
                     )
-                w_raws[(g2, half)] = w_raw
+                w_raws[(gk, h)] = w_raw
 
-        def interleave_w(g2, gk, engine_copy):
-            w_raw = w_raws[(g2, gk // 2)]
+        def interleave_w(gk, g2, engine_copy):
             w_g = g_pool.tile([P, 4 * CH], BF16, name="w_grouped", tag="g", align_bytes=64)
-            engine_copy(
-                out=w_g[:].rearrange("p (t m j) -> p t m j", t=4, j=4),
-                in_=w_raw[:, gk % 2].rearrange("p j (m t) -> p t m j", t=4),
-            )
-            groupeds[("w", g2, gk)] = w_g
+            dst = w_g[:].rearrange("p (t h a i j) -> p h t a i j", t=4, h=2, a=2, j=4)
+            for h in range(2):
+                src = w_raws[(gk, h)][:].rearrange("p j (a g i t) -> p g t a i j", a=2, g=4, t=4)
+                engine_copy(out=dst[:, h], in_=src[:, g2])
+            return w_g
 
-        def quantise_w(g2, gk):
-            w_g = groupeds.pop(("w", g2, gk))
+        def quantise_w(gk, g2, w_g):
             nc.vector.quantize_mx(
                 out=w_codes[:, gk, g2, :].bitcast(FP8X4),
                 scales=w_planes[4 * gk : P, g2, :],
                 in_=w_g[:],
             )
 
-        def stage1_slot(ci, g2, mid):
+        def stage1_pass(acc, ci, g2, t, gk):
             xc, xp = chunk_codes[(0, ci)]
+            nc.tensor.matmul_mx(
+                out=acc[:],
+                lhsT=w_codes[:, gk, g2, t * P : (t + 1) * P].bitcast(FP8X4),
+                lhsT_scale=w_planes[4 * gk : P, g2, t * P : (t + 1) * P],
+                rhs=xc[:, gk, :].bitcast(FP8X4),
+                rhs_scale=xp[4 * gk : P, :],
+                start=(gk == 0),
+                stop=(gk == NG - 1),
+            )
+
+        def stage1_slot(ci, g2):
             hb = hb_pool.tile([P, 4, CH], BF16, name="hb", tag="hb")
             for t in range(4):
-                acc = mm_pool.tile([P, CH], F32, name="acc", tag="acc")
+                acc = bank()
                 for gk in range(NG):
-                    nc.tensor.matmul_mx(
-                        out=acc[:],
-                        lhsT=w_codes[:, gk, g2, t * P : (t + 1) * P].bitcast(FP8X4),
-                        lhsT_scale=w_planes[4 * gk : P, g2, t * P : (t + 1) * P],
-                        rhs=xc[:, gk, :].bitcast(FP8X4),
-                        rhs_scale=xp[4 * gk : P, :],
-                        start=(gk == 0),
-                        stop=(gk == NG - 1),
-                    )
+                    stage1_pass(acc, ci, g2, t, gk)
                 nc.scalar.copy(out=hb[:, t, :], in_=acc[:])
-                if t == 1 and mid is not None:
-                    mid()
             return hb
+
+        def first_two_slots_with_w():
+            accs = [bank(), bank(), bank(), bank(), bank(), bank(), bank(), bank()]
+            for gk in range(NG):
+                w_gs = [
+                    interleave_w(gk, g2, (nc.vector.tensor_copy, nc.scalar.copy)[g2 % 2]) for g2 in range(NG)
+                ]
+                for g2 in range(NG):
+                    quantise_w(gk, g2, w_gs[g2])
+                for g2 in range(2):
+                    for t in range(4):
+                        stage1_pass(accs[4 * g2 + t], 0, g2, t, gk)
+            hbs = []
+            for g2 in range(2):
+                hb = hb_pool.tile([P, 4, CH], BF16, name="hb", tag="hb")
+                for t in range(4):
+                    nc.scalar.copy(out=hb[:, t, :], in_=accs[4 * g2 + t][:])
+                hbs.append(hb)
+            return hbs
 
         def interleave_h(hb):
             h_g = g_pool.tile([P, 4 * CH], BF16, name="h_grouped", tag="g", align_bytes=64)
@@ -184,7 +235,7 @@ def tile_coattentionandcombine_pa_l_kernel(tc, x1, bi_linear_w, x2, out):
             ob = ob_pool.tile([P, 4, CH], F32, name="ob", tag="ob")
             dst = out[b, lc * CH : (lc + 1) * CH, mc * CH : (mc + 1) * CH].rearrange("(t p) m -> p t m", p=P)
             for lt in range(4):
-                acc = mm_pool.tile([P, CH], F32, name="acc", tag="acc")
+                acc = bank()
                 for g2 in range(NG):
                     nc.tensor.matmul_mx(
                         out=acc[:],
@@ -201,102 +252,88 @@ def tile_coattentionandcombine_pa_l_kernel(tc, x1, bi_linear_w, x2, out):
             if not last:
                 nc.sync.dma_start(out=dst, in_=ob[:])
 
-        def both(which, chunks):
-            return [(which, ci, hf) for ci in chunks for hf in range(2)]
+        def both(which, chunks, way):
+            return [(which, ci, hf, way) for ci in chunks for hf in range(2)]
 
         slots = []
         after = {}
-        units = both(0, [0, 1])
-        n_head = len(units)
-        for b in range(B):
-            base = len(slots)
-            c0 = b * NCH
-            if b == 0:
-                slots.extend([(1, ci, g2) for g2 in range(NG) for ci in (0, 1)])
-                slots.extend([(1, ci, g2) for ci in (2, 3) for g2 in range(NG)])
-                todo = both(0, [2, 3]) + both(1, [0, 1, 2, 3])
-                first = base + 4
-            else:
-                slots.extend([(1, c0 + lc, g2) for lc in range(NCH) for g2 in range(NG)])
-                todo = both(1, [c0 + 2, c0 + 3])
-                first = base
+        units = both(0, [0], PE_WAY)
+
+        def spread(todo, base, first, span):
             for k in range(len(todo)):
-                after[first + k] = len(units) + k
+                after[base + first + (k * span) // len(todo)] = len(units) + k
             units.extend(todo)
+
+        for b in range(B):
+            c0 = b * NCH
+            base = len(slots)
+            slots.extend([(1, c0 + lc, g2) for lc in range(NCH) for g2 in range(NG)])
+            if b == 0:
+                spread(both(0, [1, 2, 3], PE_WAY) + both(1, [0, 1, 2, 3], PE_WAY), base, 1, 14)
+            else:
+                spread(both(1, [c0 + 1, c0 + 2, c0 + 3], DVE_WAY), base, 0, 16)
             base = len(slots)
             slots.extend([(2, c0 + lc, mc) for lc in range(NCH) for mc in range(NCH)])
             if b + 1 < B:
                 n0 = c0 + NCH
-                todo = both(0, [n0, n0 + 1, n0 + 2, n0 + 3]) + both(1, [n0, n0 + 1])
-                for k in range(len(todo)):
-                    after[base + k] = len(units) + k
-                units.extend(todo)
+                spread(both(0, [n0, n0 + 1, n0 + 2, n0 + 3], DVE_WAY) + both(1, [n0], DVE_WAY), base, 0, 16)
 
-        def sort_and_refill(k):
-            sort_words(units[k])
-            if k + 4 < len(units):
-                load(units[k + 4])
+        progress = {"loaded": 0}
 
-        load(units[0])
-        load(units[1])
-        load_w(0)
-        load(units[2])
-        load(units[3])
-        for g2 in range(1, NG):
-            load_w(g2)
-        sort_and_refill(0)
-        sort_and_refill(1)
-        transposes(units[0])
-        evac_transposes(units[0])
-        transposes(units[1])
-        evac_transposes(units[1])
-        interleave_w(0, 0, nc.vector.tensor_copy)
+        def ensure_loaded(upto):
+            while progress["loaded"] <= min(upto, len(units) - 1):
+                load(units[progress["loaded"]])
+                progress["loaded"] = progress["loaded"] + 1
+
+        def start_unit(k):
+            stage_a(units[k])
+            ensure_loaded(k + 4)
+
+        ensure_loaded(1)
+        for gk in range(NG):
+            load_w(gk)
+        start_unit(0)
+        start_unit(1)
+        pe_transposes(units[0])
+        pe_transposes(units[1])
         quantise_unit(units[0])
-        interleave_w(0, 1, nc.scalar.copy)
-        interleave_w(0, 2, nc.vector.tensor_copy)
         quantise_unit(units[1])
-        interleave_w(0, 3, nc.scalar.copy)
-        quantise_w(0, 0)
-        quantise_w(0, 2)
-        sort_and_refill(2)
-        transposes(units[2])
-        evac_transposes(units[2])
-        quantise_w(0, 1)
-        sort_and_refill(3)
-        transposes(units[3])
-        evac_transposes(units[3])
-        quantise_w(0, 3)
-        quantise_unit(units[2])
-        quantise_unit(units[3])
 
-        for n in range(len(slots)):
+        hbs = first_two_slots_with_w()
+        start_unit(after[1])
+        pe_transposes(units[after[1]])
+        pend_q = units[after[1]]
+        h_g = interleave_h(hbs[0])
+        start_unit(after[2])
+        quantise_h(0, 0, h_g)
+        pend_h = (0, 1, hbs[1])
+        for n in range(2, len(slots)):
             kind, ci, sub = slots[n]
-            w_job = None
-            if n < 2 * (NG - 1):
-                w_job = (n // 2 + 1, 2 * (n % 2))
-            if w_job is not None:
-                interleave_w(w_job[0], w_job[1], nc.vector.tensor_copy)
-            if (n + 1) in after:
-                sort_and_refill(after[n + 1])
-            if w_job is not None:
-                quantise_w(w_job[0], w_job[1])
+            unit = None
+            if n in after:
+                unit = units[after[n]]
+            if (n + 1) in after and units[after[n + 1]][3] == DVE_WAY:
+                start_unit(after[n + 1])
+            h_g = None
+            if pend_h is not None:
+                h_g = interleave_h(pend_h[2])
+            if unit is not None and unit[3] == DVE_WAY:
+                dve_transpose(unit)
+            if (n + 1) in after and units[after[n + 1]][3] == PE_WAY:
+                start_unit(after[n + 1])
+            if pend_q is not None:
+                quantise_unit(pend_q)
+                pend_q = None
+            if pend_h is not None:
+                quantise_h(pend_h[0], pend_h[1], h_g)
+                pend_h = None
+            if unit is not None and unit[3] == DVE_WAY:
+                dve_regroup(unit)
 
             if kind == 1:
-                mid = None
-                if w_job is not None:
-                    mid = lambda wj=w_job: interleave_w(wj[0], wj[1] + 1, nc.scalar.copy)
-                hb = stage1_slot(ci, sub, mid)
+                pend_h = (ci, sub, stage1_slot(ci, sub))
             else:
                 stage2_slot(ci, sub, n == len(slots) - 1)
-            if w_job is not None:
-                quantise_w(w_job[0], w_job[1] + 1)
-
-            if n in after:
-                transposes(units[after[n]])
-                evac_transposes(units[after[n]])
-            if kind == 1:
-                h_g = interleave_h(hb)
-            if n in after:
-                quantise_unit(units[after[n]])
-            if kind == 1:
-                quantise_h(ci, sub, h_g)
+            if unit is not None and unit[3] == PE_WAY:
+                pe_transposes(unit)
+            pend_q = unit

@@ -20,6 +20,8 @@ NG = 4
 NCH = L // CH
 PE_WAY = 0
 DVE_WAY = 1
+LAG = 2
+LATE_SPAN = 60
 
 
 def tile_coattentionandcombine_pa_l_kernel(tc, x1, bi_linear_w, x2, out):
@@ -29,8 +31,8 @@ def tile_coattentionandcombine_pa_l_kernel(tc, x1, bi_linear_w, x2, out):
     with ExitStack() as ctx:
         const = ctx.enter_context(tc.tile_pool(name="const", bufs=1))
         keep = ctx.enter_context(tc.tile_pool(name="keep", bufs=1))
-        codes_pool = ctx.enter_context(tc.tile_pool(name="codes", bufs=11))
-        x_pool = ctx.enter_context(tc.tile_pool(name="xprep", bufs=8))
+        codes_pool = ctx.enter_context(tc.tile_pool(name="codes", bufs=12))
+        x_pool = ctx.enter_context(tc.tile_pool(name="xprep", bufs=7))
         g_pool = ctx.enter_context(tc.tile_pool(name="grouped", bufs=4))
         hb_pool = ctx.enter_context(tc.tile_pool(name="hb", bufs=2))
         ob_pool = ctx.enter_context(tc.tile_pool(name="ob", bufs=2))
@@ -207,6 +209,10 @@ def tile_coattentionandcombine_pa_l_kernel(tc, x1, bi_linear_w, x2, out):
                 for g2 in range(2):
                     for t in range(4):
                         stage1_pass(accs[4 * g2 + t], 0, g2, t, gk)
+                if gk + 2 < NG:
+                    load_w(gk + 2)
+                elif gk + 2 == NG:
+                    ensure_loaded(4)
             hbs = []
             for g2 in range(2):
                 hb = hb_pool.tile([P, 4, CH], BF16, name="hb", tag="hb")
@@ -259,24 +265,29 @@ def tile_coattentionandcombine_pa_l_kernel(tc, x1, bi_linear_w, x2, out):
         after = {}
         units = both(0, [0], PE_WAY)
 
-        def spread(todo, base, first, span):
+        def spread(todo, first, span):
             for k in range(len(todo)):
-                after[base + first + (k * span) // len(todo)] = len(units) + k
+                after[first + (k * span) // len(todo)] = len(units) + k
             units.extend(todo)
 
-        for b in range(B):
+        n_chunks = B * NCH
+        for ci in range(LAG):
+            slots.extend([(1, ci, g2) for g2 in range(NG)])
+        for ci in range(n_chunks - LAG):
+            for q in range(NG):
+                slots.append((1, ci + LAG, q))
+                slots.append((2, ci, q))
+        for ci in range(n_chunks - LAG, n_chunks):
+            slots.extend([(2, ci, mc) for mc in range(NCH)])
+        early = both(0, [1, 2], PE_WAY) + both(1, [0, 1, 2, 3], PE_WAY) + both(0, [3], PE_WAY)
+        spread(early, 1, len(early))
+        late = []
+        for b in range(1, B):
             c0 = b * NCH
-            base = len(slots)
-            slots.extend([(1, c0 + lc, g2) for lc in range(NCH) for g2 in range(NG)])
-            if b == 0:
-                spread(both(0, [1, 2, 3], PE_WAY) + both(1, [0, 1, 2, 3], PE_WAY), base, 1, 14)
-            else:
-                spread(both(1, [c0 + 1, c0 + 2, c0 + 3], DVE_WAY), base, 0, 16)
-            base = len(slots)
-            slots.extend([(2, c0 + lc, mc) for lc in range(NCH) for mc in range(NCH)])
-            if b + 1 < B:
-                n0 = c0 + NCH
-                spread(both(0, [n0, n0 + 1, n0 + 2, n0 + 3], DVE_WAY) + both(1, [n0], DVE_WAY), base, 0, 16)
+            late.extend(both(0, [c0, c0 + 1, c0 + 2], DVE_WAY))
+            late.extend(both(1, [c0, c0 + 1, c0 + 2, c0 + 3], DVE_WAY))
+            late.extend(both(0, [c0 + 3], DVE_WAY))
+        spread(late, 1 + len(early), LATE_SPAN)
 
         progress = {"loaded": 0}
 
@@ -287,15 +298,15 @@ def tile_coattentionandcombine_pa_l_kernel(tc, x1, bi_linear_w, x2, out):
 
         def start_unit(k):
             stage_a(units[k])
-            ensure_loaded(k + 4)
+            ensure_loaded(k + 3)
 
         ensure_loaded(1)
-        for gk in range(NG):
-            load_w(gk)
-        start_unit(0)
-        start_unit(1)
+        load_w(0)
+        stage_a(units[0])
+        stage_a(units[1])
         pe_transposes(units[0])
         pe_transposes(units[1])
+        load_w(1)
         quantise_unit(units[0])
         quantise_unit(units[1])
 

@@ -21,7 +21,8 @@ NCH = L // CH
 PE_WAY = 0
 DVE_WAY = 1
 LAG = 2
-LATE_SPAN = 60
+LATE_SPAN = 64
+PE_EVERY = 0
 
 
 def tile_coattentionandcombine_pa_l_kernel(tc, x1, bi_linear_w, x2, out):
@@ -72,7 +73,7 @@ def tile_coattentionandcombine_pa_l_kernel(tc, x1, bi_linear_w, x2, out):
                 nc.sync.dma_start(
                     out=raw[:], in_=xs[which][b, t0 : t0 + UT, :].rearrange("(s p) k -> p s k", p=P)
                 )
-            else:
+            elif which == 1:
                 raw = x_tile([P, 8, CH], BF16)
                 for a in range(4):
                     quadrant_queue(a).dma_start(
@@ -81,6 +82,17 @@ def tile_coattentionandcombine_pa_l_kernel(tc, x1, bi_linear_w, x2, out):
                             "(s j) k -> j s k", j=Q
                         ),
                     )
+            else:
+                raw = x_tile([P, 2, 16, P], BF16)
+                for g in range(2):
+                    for a in range(4):
+                        k0 = (2 * hf + g) * 512 + a * P
+                        quadrant_queue(a).dma_start(
+                            out=raw[a * Q : (a + 1) * Q, g],
+                            in_=xs[which][b, c * CH : (c + 1) * CH, k0 : k0 + P].rearrange(
+                                "(s j) k -> j s k", j=Q
+                            ),
+                        )
             stage[("raw", u)] = raw
 
         def stage_a(u):
@@ -90,12 +102,21 @@ def tile_coattentionandcombine_pa_l_kernel(tc, x1, bi_linear_w, x2, out):
                 words = raw[:].bitcast(F32)
                 dst = srt[:].rearrange("p (s r) -> p s r", s=2)
                 for s2 in range(2):
-                    nc.vector.tensor_copy(
-                        out=dst[:, s2, :].rearrange("p (g u a i) -> p g u a i", g=4, u=2, a=4),
-                        in_=words[:, s2, :].rearrange("p (a g i u) -> p g u a i", a=4, g=4, u=2),
-                    )
+                    if u[0] == 1:
+                        nc.vector.tensor_copy(
+                            out=dst[:, s2, :].rearrange("p (g u a i) -> p g u a i", g=4, u=2, a=4),
+                            in_=words[:, s2, :].rearrange("p (a g i u) -> p g u a i", a=4, g=4, u=2),
+                        )
+                    else:
+                        nc.vector.tensor_copy(
+                            out=dst[:, s2, :].rearrange("p (g u q) -> p g u q", g=4, u=2),
+                            in_=words[:, s2, :].rearrange("p (g q u) -> p g u q", g=4, u=2),
+                        )
             else:
-                words = raw[:].rearrange("p s k -> p (s k)").bitcast(F32)
+                if u[0] == 1:
+                    words = raw[:].rearrange("p s k -> p (s k)").bitcast(F32)
+                else:
+                    words = raw[:].rearrange("p g s k -> p (g s k)").bitcast(F32)
                 nc.scalar.copy(
                     out=srt[:].rearrange("p (r u i) -> p r u i", u=2, i=Q),
                     in_=words.rearrange("p (r i u) -> p r u i", i=Q, u=2),
@@ -129,11 +150,18 @@ def tile_coattentionandcombine_pa_l_kernel(tc, x1, bi_linear_w, x2, out):
 
         def dve_regroup(u):
             turned = stage.pop(("turned", u))
-            grouped = x_tile([P, NG, 4 * UT], BF16)
-            nc.vector.tensor_copy(
-                out=grouped[:].bitcast(F32).rearrange("p g (s j u) -> p g s j u", s=8, u=2),
-                in_=turned[:].rearrange("p (s g u j) -> p g s j u", s=8, g=4, u=2),
-            )
+            if u[0] == 1:
+                grouped = x_tile([P, NG, 4 * UT], BF16)
+                nc.vector.tensor_copy(
+                    out=grouped[:].bitcast(F32).rearrange("p g (s j u) -> p g s j u", s=8, u=2),
+                    in_=turned[:].rearrange("p (s g u j) -> p g s j u", s=8, g=4, u=2),
+                )
+            else:
+                grouped = x_tile([P, 2, 4 * CH], BF16)
+                nc.vector.tensor_copy(
+                    out=grouped[:].bitcast(F32).rearrange("p g (s j u) -> p (g s) j u", s=16, u=2),
+                    in_=turned[:].rearrange("p (r u j) -> p r j u", u=2, j=Q),
+                )
             stage[("grouped", u)] = grouped
 
         def quantise_unit(u):
@@ -142,6 +170,13 @@ def tile_coattentionandcombine_pa_l_kernel(tc, x1, bi_linear_w, x2, out):
                 new_codes((which, ci))
             c, s = chunk_codes[(which, ci)]
             grouped = stage.pop(("grouped", u))
+            if which == 0 and way == DVE_WAY:
+                for g2 in range(2):
+                    g = 2 * hf + g2
+                    nc.vector.quantize_mx(
+                        out=c[:, g, :].bitcast(FP8X4), scales=s[4 * g : P, :], in_=grouped[:, g2, :]
+                    )
+                return
             for g in range(NG):
                 nc.vector.quantize_mx(
                     out=c[:, g, hf * UT : (hf + 1) * UT].bitcast(FP8X4),
@@ -152,14 +187,12 @@ def tile_coattentionandcombine_pa_l_kernel(tc, x1, bi_linear_w, x2, out):
         def load_w(gk):
             for h in range(2):
                 w_raw = codes_pool.tile([P, 4, 1024], BF16, name="w_raw", tag="codes", align_bytes=64)
-                for a in range(4):
-                    r0 = a * 512 + gk * P
-                    quadrant_queue(a).dma_start(
-                        out=w_raw[a * Q : (a + 1) * Q],
-                        in_=bi_linear_w[r0 : r0 + P, h * 1024 : (h + 1) * 1024].rearrange(
-                            "(i j) c -> i j c", j=4
-                        ),
-                    )
+                nc.sync.dma_start(
+                    out=w_raw[:],
+                    in_=bi_linear_w[gk * 512 : (gk + 1) * 512, h * 1024 : (h + 1) * 1024].rearrange(
+                        "(p j) c -> p j c", j=4
+                    ),
+                )
                 w_raws[(gk, h)] = w_raw
 
         def interleave_w(gk, g2, engine_copy):
@@ -287,6 +320,11 @@ def tile_coattentionandcombine_pa_l_kernel(tc, x1, bi_linear_w, x2, out):
             late.extend(both(0, [c0, c0 + 1, c0 + 2], DVE_WAY))
             late.extend(both(1, [c0, c0 + 1, c0 + 2, c0 + 3], DVE_WAY))
             late.extend(both(0, [c0 + 3], DVE_WAY))
+        if PE_EVERY:
+            late = [
+                (late[k][0], late[k][1], late[k][2], PE_WAY if k % PE_EVERY == PE_EVERY - 1 else DVE_WAY)
+                for k in range(len(late))
+            ]
         spread(late, 1 + len(early), LATE_SPAN)
 
         progress = {"loaded": 0}
@@ -328,13 +366,13 @@ def tile_coattentionandcombine_pa_l_kernel(tc, x1, bi_linear_w, x2, out):
             h_g = None
             if pend_h is not None:
                 h_g = interleave_h(pend_h[2])
+            if pend_q is not None:
+                quantise_unit(pend_q)
+                pend_q = None
             if unit is not None and unit[3] == DVE_WAY:
                 dve_transpose(unit)
             if (n + 1) in after and units[after[n + 1]][3] == PE_WAY:
                 start_unit(after[n + 1])
-            if pend_q is not None:
-                quantise_unit(pend_q)
-                pend_q = None
             if pend_h is not None:
                 quantise_h(pend_h[0], pend_h[1], h_g)
                 pend_h = None

@@ -325,7 +325,7 @@ def tile_coattentionandcombine_pa_l_kernel(tc, x1, bi_linear_w, x2, out):
                 (late[k][0], late[k][1], late[k][2], PE_WAY if k % PE_EVERY == PE_EVERY - 1 else DVE_WAY)
                 for k in range(len(late))
             ]
-        spread(late, 1 + len(early), LATE_SPAN)
+        spread(late, 2 + len(early), LATE_SPAN)
 
         progress = {"loaded": 0}
 

from contextlib import ExitStack

import concourse.mybir as mybir
from concourse.masks import make_identity

B, L, D = 3, 2048, 2048
FLOPS = 2 * 2 * B * L * D * D

F32 = mybir.dt.float32
BF16 = mybir.dt.bfloat16
U32 = mybir.dt.uint32
U8 = mybir.dt.uint8
FP8X4 = mybir.dt.float8_e4m3fn_x4

P = 128
Q = 32
CH = 512
UT = 256
NG = 4
NCH = L // CH
PE_WAY = 0
DVE_WAY = 1
LAG = 2
LATE_SPAN = 64
PE_EVERY = 0


def tile_coattentionandcombine_pa_l_kernel(tc, x1, bi_linear_w, x2, out):
    nc = tc.nc
    xs = (x1, x2)

    with ExitStack() as ctx:
        const = ctx.enter_context(tc.tile_pool(name="const", bufs=1))
        keep = ctx.enter_context(tc.tile_pool(name="keep", bufs=1))
        codes_pool = ctx.enter_context(tc.tile_pool(name="codes", bufs=12))
        x_pool = ctx.enter_context(tc.tile_pool(name="xprep", bufs=7))
        g_pool = ctx.enter_context(tc.tile_pool(name="grouped", bufs=4))
        hb_pool = ctx.enter_context(tc.tile_pool(name="hb", bufs=2))
        ob_pool = ctx.enter_context(tc.tile_pool(name="ob", bufs=2))
        psum = ctx.enter_context(tc.psum_pool(name="psum", bufs=8))
        ctx.enter_context(tc.manual_schedule())

        ident = const.tile([P, P], F32, name="ident")
        make_identity(nc, ident[:])

        w_codes = keep.tile([P, NG, NG, CH], U32, name="w_codes", align_bytes=64)
        w_planes = keep.tile([P, NG, CH], U8, name="w_planes", align_bytes=64)

        stage = {}
        chunk_codes = {}
        w_raws = {}

        def new_codes(key):
            c = codes_pool.tile([P, NG, CH], U32, name="codes", tag="codes", align_bytes=64)
            s = codes_pool.tile([P, CH], U8, name="planes", tag="planes", align_bytes=64)
            chunk_codes[key] = (c, s)

        def x_tile(shape, dtype):
            return x_pool.tile(shape, dtype, name="xt", tag="xt", align_bytes=64)

        def bank():
            return psum.tile([P, CH], F32, name="bank", tag="bank")

        def quadrant_queue(a):
            return (nc.sync, nc.scalar)[a // 2]

        def load(u):
            which, ci, hf, way = u
            b, c = divmod(ci, NCH)
            t0 = c * CH + hf * UT
            if way == PE_WAY:
                raw = x_tile([P, 2, D], BF16)
                nc.sync.dma_start(
                    out=raw[:], in_=xs[which][b, t0 : t0 + UT, :].rearrange("(s p) k -> p s k", p=P)
                )
            elif which == 1:
                raw = x_tile([P, 8, CH], BF16)
                for a in range(4):
                    quadrant_queue(a).dma_start(
                        out=raw[a * Q : (a + 1) * Q],
                        in_=xs[which][b, t0 : t0 + UT, a * CH : (a + 1) * CH].rearrange(
                            "(s j) k -> j s k", j=Q
                        ),
                    )
            else:
                raw = x_tile([P, 2, 16, P], BF16)
                for g in range(2):
                    for a in range(4):
                        k0 = (2 * hf + g) * 512 + a * P
                        quadrant_queue(a).dma_start(
                            out=raw[a * Q : (a + 1) * Q, g],
                            in_=xs[which][b, c * CH : (c + 1) * CH, k0 : k0 + P].rearrange(
                                "(s j) k -> j s k", j=Q
                            ),
                        )
            stage[("raw", u)] = raw

        def stage_a(u):
            raw = stage.pop(("raw", u))
            srt = x_tile([P, 2048], F32)
            if u[3] == PE_WAY:
                words = raw[:].bitcast(F32)
                dst = srt[:].rearrange("p (s r) -> p s r", s=2)
                for s2 in range(2):
                    if u[0] == 1:
                        nc.vector.tensor_copy(
                            out=dst[:, s2, :].rearrange("p (g u a i) -> p g u a i", g=4, u=2, a=4),
                            in_=words[:, s2, :].rearrange("p (a g i u) -> p g u a i", a=4, g=4, u=2),
                        )
                    else:
                        nc.vector.tensor_copy(
                            out=dst[:, s2, :].rearrange("p (g u q) -> p g u q", g=4, u=2),
                            in_=words[:, s2, :].rearrange("p (g q u) -> p g u q", g=4, u=2),
                        )
            else:
                if u[0] == 1:
                    words = raw[:].rearrange("p s k -> p (s k)").bitcast(F32)
                else:
                    words = raw[:].rearrange("p g s k -> p (g s k)").bitcast(F32)
                nc.scalar.copy(
                    out=srt[:].rearrange("p (r u i) -> p r u i", u=2, i=Q),
                    in_=words.rearrange("p (r i u) -> p r u i", i=Q, u=2),
                )
            stage[("srt", u)] = srt

        def pe_transposes(u):
            srt = stage.pop(("srt", u))[:].rearrange("p (s g u q) -> p s g u q", s=2, g=4, u=2)
            grouped = x_tile([P, NG, 4 * UT], BF16)
            gw = grouped[:].bitcast(F32)
            got = []
            for g in range(NG):
                tp = bank()
                tpv = tp[:].rearrange("p (s u c) -> p s u c", s=2, u=2)
                for s2 in range(2):
                    for uu in range(2):
                        nc.tensor.transpose(tpv[:, s2, uu, :], srt[:, s2, g, uu, :], ident[:])
                got.append(tpv)
            for g in range(NG):
                nc.scalar.copy(
                    out=gw[:, g, :].rearrange("p (s c u) -> p s c u", s=2, u=2),
                    in_=got[g].rearrange("p s u c -> p s c u"),
                )
            stage[("grouped", u)] = grouped

        def dve_transpose(u):
            srt = stage.pop(("srt", u))
            turned = x_tile([P, 2048], F32)
            nc.vector.transpose(out=turned[:], in_=srt[:])
            stage[("turned", u)] = turned

        def dve_regroup(u):
            turned = stage.pop(("turned", u))
            if u[0] == 1:
                grouped = x_tile([P, NG, 4 * UT], BF16)
                nc.vector.tensor_copy(
                    out=grouped[:].bitcast(F32).rearrange("p g (s j u) -> p g s j u", s=8, u=2),
                    in_=turned[:].rearrange("p (s g u j) -> p g s j u", s=8, g=4, u=2),
                )
            else:
                grouped = x_tile([P, 2, 4 * CH], BF16)
                nc.vector.tensor_copy(
                    out=grouped[:].bitcast(F32).rearrange("p g (s j u) -> p (g s) j u", s=16, u=2),
                    in_=turned[:].rearrange("p (r u j) -> p r j u", u=2, j=Q),
                )
            stage[("grouped", u)] = grouped

        def quantise_unit(u):
            which, ci, hf, way = u
            if hf == 0:
                new_codes((which, ci))
            c, s = chunk_codes[(which, ci)]
            grouped = stage.pop(("grouped", u))
            if which == 0 and way == DVE_WAY:
                for g2 in range(2):
                    g = 2 * hf + g2
                    nc.vector.quantize_mx(
                        out=c[:, g, :].bitcast(FP8X4), scales=s[4 * g : P, :], in_=grouped[:, g2, :]
                    )
                return
            for g in range(NG):
                nc.vector.quantize_mx(
                    out=c[:, g, hf * UT : (hf + 1) * UT].bitcast(FP8X4),
                    scales=s[4 * g : P, hf * UT : (hf + 1) * UT],
                    in_=grouped[:, g, :],
                )

        def load_w(gk):
            for h in range(2):
                w_raw = codes_pool.tile([P, 4, 1024], BF16, name="w_raw", tag="codes", align_bytes=64)
                nc.sync.dma_start(
                    out=w_raw[:],
                    in_=bi_linear_w[gk * 512 : (gk + 1) * 512, h * 1024 : (h + 1) * 1024].rearrange(
                        "(p j) c -> p j c", j=4
                    ),
                )
                w_raws[(gk, h)] = w_raw

        def interleave_w(gk, g2, engine_copy):
            w_g = g_pool.tile([P, 4 * CH], BF16, name="w_grouped", tag="g", align_bytes=64)
            dst = w_g[:].rearrange("p (t h a i j) -> p h t a i j", t=4, h=2, a=2, j=4)
            for h in range(2):
                src = w_raws[(gk, h)][:].rearrange("p j (a g i t) -> p g t a i j", a=2, g=4, t=4)
                engine_copy(out=dst[:, h], in_=src[:, g2])
            return w_g

        def quantise_w(gk, g2, w_g):
            nc.vector.quantize_mx(
                out=w_codes[:, gk, g2, :].bitcast(FP8X4),
                scales=w_planes[4 * gk : P, g2, :],
                in_=w_g[:],
            )

        def stage1_pass(acc, ci, g2, t, gk):
            xc, xp = chunk_codes[(0, ci)]
            nc.tensor.matmul_mx(
                out=acc[:],
                lhsT=w_codes[:, gk, g2, t * P : (t + 1) * P].bitcast(FP8X4),
                lhsT_scale=w_planes[4 * gk : P, g2, t * P : (t + 1) * P],
                rhs=xc[:, gk, :].bitcast(FP8X4),
                rhs_scale=xp[4 * gk : P, :],
                start=(gk == 0),
                stop=(gk == NG - 1),
            )

        def stage1_slot(ci, g2):
            hb = hb_pool.tile([P, 4, CH], BF16, name="hb", tag="hb")
            for t in range(4):
                acc = bank()
                for gk in range(NG):
                    stage1_pass(acc, ci, g2, t, gk)
                nc.scalar.copy(out=hb[:, t, :], in_=acc[:])
            return hb

        def first_two_slots_with_w():
            accs = [bank(), bank(), bank(), bank(), bank(), bank(), bank(), bank()]
            for gk in range(NG):
                w_gs = [
                    interleave_w(gk, g2, (nc.vector.tensor_copy, nc.scalar.copy)[g2 % 2]) for g2 in range(NG)
                ]
                for g2 in range(NG):
                    quantise_w(gk, g2, w_gs[g2])
                for g2 in range(2):
                    for t in range(4):
                        stage1_pass(accs[4 * g2 + t], 0, g2, t, gk)
                if gk + 2 < NG:
                    load_w(gk + 2)
                elif gk + 2 == NG:
                    ensure_loaded(4)
            hbs = []
            for g2 in range(2):
                hb = hb_pool.tile([P, 4, CH], BF16, name="hb", tag="hb")
                for t in range(4):
                    nc.scalar.copy(out=hb[:, t, :], in_=accs[4 * g2 + t][:])
                hbs.append(hb)
            return hbs

        def interleave_h(hb):
            h_g = g_pool.tile([P, 4 * CH], BF16, name="h_grouped", tag="g", align_bytes=64)
            nc.vector.tensor_copy(
                out=h_g[:].rearrange("p (c t) -> p c t", t=4), in_=hb[:].rearrange("p t c -> p c t")
            )
            return h_g

        def quantise_h(ci, g2, h_g):
            if (2, ci) not in chunk_codes:
                new_codes((2, ci))
            c, s = chunk_codes[(2, ci)]
            nc.vector.quantize_mx(out=c[:, g2, :].bitcast(FP8X4), scales=s[4 * g2 : P, :], in_=h_g[:])

        def stage2_slot(ci, mc, last):
            b, lc = divmod(ci, NCH)
            hc, hp = chunk_codes[(2, ci)]
            xc, xp = chunk_codes[(1, b * NCH + mc)]
            ob = ob_pool.tile([P, 4, CH], F32, name="ob", tag="ob")
            dst = out[b, lc * CH : (lc + 1) * CH, mc * CH : (mc + 1) * CH].rearrange("(t p) m -> p t m", p=P)
            for lt in range(4):
                acc = bank()
                for g2 in range(NG):
                    nc.tensor.matmul_mx(
                        out=acc[:],
                        lhsT=hc[:, g2, lt * P : (lt + 1) * P].bitcast(FP8X4),
                        lhsT_scale=hp[4 * g2 : P, lt * P : (lt + 1) * P],
                        rhs=xc[:, g2, :].bitcast(FP8X4),
                        rhs_scale=xp[4 * g2 : P, :],
                        start=(g2 == 0),
                        stop=(g2 == NG - 1),
                    )
                nc.scalar.copy(out=ob[:, lt, :], in_=acc[:])
                if last:
                    nc.sync.dma_start(out=dst[:, lt, :], in_=ob[:, lt, :])
            if not last:
                nc.sync.dma_start(out=dst, in_=ob[:])

        def both(which, chunks, way):
            return [(which, ci, hf, way) for ci in chunks for hf in range(2)]

        slots = []
        after = {}
        units = both(0, [0], PE_WAY)

        def spread(todo, first, span):
            for k in range(len(todo)):
                after[first + (k * span) // len(todo)] = len(units) + k
            units.extend(todo)

        n_chunks = B * NCH
        for ci in range(LAG):
            slots.extend([(1, ci, g2) for g2 in range(NG)])
        for ci in range(n_chunks - LAG):
            for q in range(NG):
                slots.append((1, ci + LAG, q))
                slots.append((2, ci, q))
        for ci in range(n_chunks - LAG, n_chunks):
            slots.extend([(2, ci, mc) for mc in range(NCH)])
        early = both(0, [1, 2], PE_WAY) + both(1, [0, 1, 2, 3], PE_WAY) + both(0, [3], PE_WAY)
        spread(early, 1, len(early))
        late = []
        for b in range(1, B):
            c0 = b * NCH
            late.extend(both(0, [c0, c0 + 1, c0 + 2], DVE_WAY))
            late.extend(both(1, [c0, c0 + 1, c0 + 2, c0 + 3], DVE_WAY))
            late.extend(both(0, [c0 + 3], DVE_WAY))
        if PE_EVERY:
            late = [
                (late[k][0], late[k][1], late[k][2], PE_WAY if k % PE_EVERY == PE_EVERY - 1 else DVE_WAY)
                for k in range(len(late))
            ]
        spread(late, 2 + len(early), LATE_SPAN)

        progress = {"loaded": 0}

        def ensure_loaded(upto):
            while progress["loaded"] <= min(upto, len(units) - 1):
                load(units[progress["loaded"]])
                progress["loaded"] = progress["loaded"] + 1

        def start_unit(k):
            stage_a(units[k])
            ensure_loaded(k + 3)

        ensure_loaded(1)
        load_w(0)
        stage_a(units[0])
        stage_a(units[1])
        pe_transposes(units[0])
        pe_transposes(units[1])
        load_w(1)
        quantise_unit(units[0])
        quantise_unit(units[1])

        hbs = first_two_slots_with_w()
        start_unit(after[1])
        pe_transposes(units[after[1]])
        pend_q = units[after[1]]
        h_g = interleave_h(hbs[0])
        start_unit(after[2])
        quantise_h(0, 0, h_g)
        pend_h = (0, 1, hbs[1])
        for n in range(2, len(slots)):
            kind, ci, sub = slots[n]
            unit = None
            if n in after:
                unit = units[after[n]]
            if (n + 1) in after and units[after[n + 1]][3] == DVE_WAY:
                start_unit(after[n + 1])
            h_g = None
            if pend_h is not None:
                h_g = interleave_h(pend_h[2])
            if pend_q is not None:
                quantise_unit(pend_q)
                pend_q = None
            if unit is not None and unit[3] == DVE_WAY:
                dve_transpose(unit)
            if (n + 1) in after and units[after[n + 1]][3] == PE_WAY:
                start_unit(after[n + 1])
            if pend_h is not None:
                quantise_h(pend_h[0], pend_h[1], h_g)
                pend_h = None
            if unit is not None and unit[3] == DVE_WAY:
                dve_regroup(unit)

            if kind == 1:
                pend_h = (ci, sub, stage1_slot(ci, sub))
            else:
                stage2_slot(ci, sub, n == len(slots) - 1)
            if unit is not None and unit[3] == PE_WAY:
                pe_transposes(unit)
            pend_q = unit
